import numpy as np
import ml_dtypes


def mxq(x, axis, fmt="e4m3"):
    dtype, down = {"e4m3": (ml_dtypes.float8_e4m3fn, 7), "e5m2": (ml_dtypes.float8_e5m2, 14)}[fmt]
    v = np.moveaxis(np.asarray(x, np.float32).astype(ml_dtypes.bfloat16).astype(np.float64), axis, -1)
    blocks = v.reshape(v.shape[:-1] + (-1, 32))
    amax = np.abs(blocks).max(-1, keepdims=True)
    byte = np.maximum(np.where(amax > 0, np.frexp(amax)[1] - 1 + 127, 0) - down, 1)
    scale = np.exp2(byte - 127.0)
    codes = (blocks / scale).astype(np.float32).astype(dtype).astype(np.float64)
    return np.moveaxis((codes * scale).reshape(v.shape), -1, axis)


WIDE = False


def mx_kscale(k):
    if not WIDE:
        return np.ones(k)
    levels = np.array([30, -30])
    if k % 512:
        return np.exp2(np.random.permutation(np.resize(levels, k // 32))).repeat(32)
    a = np.empty((k // 512, 16))
    for p in range(k // 512):
        a[p, :8] = np.random.permutation(np.resize(levels, 8))
        for g in range(8):
            far = levels[np.abs(levels - a[p, g]) >= 10]
            a[p, g + 8] = far[np.random.randint(len(far))]
    return np.exp2(a.ravel()).repeat(32)


BF16 = ml_dtypes.bfloat16


def bf(x):
    return np.asarray(x, np.float32).astype(BF16)


def f64(x):
    return np.asarray(x).astype(np.float64)


B, S, H, E, D, TRAIN_LEN = 1, 1024, 1024, 1536, 128, 512


def silu(v):
    return v / (1.0 + np.exp(-v))


def apply_rotary(x, sin, cos):
    x1, x2 = x[..., 0::2], x[..., 1::2]
    return np.concatenate([x1 * cos - x2 * sin, x1 * sin + x2 * cos], axis=-1)


def setup_inputs():
    s = mx_kscale(H)
    pos = np.arange(S)[:, None]
    inv = np.exp(-np.arange(0, D, 2) / D * np.log(10000.0))
    ang = pos * inv[None, :]
    return {"hidden_states": bf(np.random.standard_normal((B, S, H)) * s),
            "sin": bf(np.sin(ang)[None]),
            "cos": bf(np.cos(ang)[None]),
            "W_i": bf(np.random.standard_normal((H, 2 * E + D)) / np.sqrt(H) / s[:, None]),
            "q_scale": bf(1.0 + 0.1 * np.random.standard_normal(D)),
            "k_scale": bf(1.0 + 0.1 * np.random.standard_normal(D))}


def reference(hidden_states, sin, cos, W_i, q_scale, k_scale):
    x = silu(mxq(f64(hidden_states), 2, "e5m2") @ mxq(f64(W_i), 0, "e4m3"))
    u, v, qk = np.split(x, [E, 2 * E], axis=-1)
    sn, cs = f64(sin), f64(cos)
    q = apply_rotary(qk * f64(q_scale), sn, cs)
    k = apply_rotary(qk * f64(k_scale), sn, cs)
    return u, v, q, k

@@ -1,0 +1,224 @@
+from contextlib import ExitStack
+
+import concourse.mybir as mybir
+from concourse.masks import make_identity
+
+S, H, E, D = 1024, 1024, 1536, 128
+FLOPS = 2 * S * H * (2 * E + D)
+
+F32 = mybir.dt.float32
+BF16 = mybir.dt.bfloat16
+U32 = mybir.dt.uint32
+U8 = mybir.dt.uint8
+E4M3X4 = mybir.dt.float8_e4m3fn_x4
+E5M2X4 = mybir.dt.float8_e5m2_x4
+SILU = mybir.ActivationFunctionType.Silu
+MULT = mybir.AluOpType.mult
+ADD = mybir.AluOpType.add
+SUB = mybir.AluOpType.subtract
+
+P = 128
+PACK = 4
+K_PASS = P * PACK
+PASSES = H // K_PASS
+TILES = S // P
+CHUNK = 512
+CHUNKS = E // CHUNK
+HALF = D // 2
+X_LOADS = ((0, 2), (2, 4), (4, 8))
+W_LOADS = ((0, CHUNK), (CHUNK, E), (E, 2 * E + D))
+QK = 2 * CHUNKS
+
+
+def tile_gatedattentionunit_pa_kernel(
+    tc, hidden_states, sin, cos, W_i, q_scale, k_scale, out_0, out_1, out_2, out_3
+):
+    nc = tc.nc
+
+    def by_token(ap):
+        return ap.flatten_outer_dims().rearrange("(p i) c -> p i c", i=TILES)
+
+    with ExitStack() as ctx:
+        keep = ctx.enter_context(tc.tile_pool(name="keep", bufs=1))
+        ring = ctx.enter_context(tc.tile_pool(name="ring", bufs=1))
+        psum = ctx.enter_context(tc.psum_pool(name="psum", bufs=1))
+        ctx.enter_context(tc.manual_schedule())
+
+        ident = keep.tile([P, P], F32)
+        make_identity(nc, ident[:])
+        ones = keep.tile([P, P], BF16)
+        nc.gpsimd.memset(ones[:], 1.0)
+        gain_rows = keep.tile([P, 2 * D], BF16)
+        nc.gpsimd.memset(gain_rows[:], 0.0)
+
+        x_rows = {}
+        for lo, hi in X_LOADS:
+            x_raw = keep.tile([P, hi - lo, H], BF16, name="x_raw%d" % lo)
+            nc.sync.dma_start(out=x_raw[:], in_=by_token(hidden_states)[:, lo:hi, :])
+            for i in range(lo, hi):
+                x_rows[i] = x_raw[:, i - lo, :]
+        w_loaded = []
+        for lo, hi in W_LOADS:
+            for g in range(PASSES):
+                w_raw = keep.tile([P, PACK, hi - lo], BF16, name="w_raw%d_%d" % (lo, g))
+                nc.sync.dma_start(
+                    out=w_raw[:],
+                    in_=W_i[g * K_PASS : (g + 1) * K_PASS, lo:hi].rearrange("(p j) w -> p j w", j=PACK),
+                )
+                w_loaded.append((lo, hi, g, w_raw))
+        sin_sb = keep.tile([P, TILES, HALF], BF16)
+        cos_sb = keep.tile([P, TILES, HALF], BF16)
+        nc.sync.dma_start(out=sin_sb[:], in_=by_token(sin))
+        nc.sync.dma_start(out=cos_sb[:], in_=by_token(cos))
+        nc.sync.dma_start(out=gain_rows[0:1, 0:D], in_=q_scale.rearrange("(o d) -> o d", o=1))
+        nc.sync.dma_start(out=gain_rows[0:1, D : 2 * D], in_=k_scale.rearrange("(o d) -> o d", o=1))
+
+        x_grouped = {}
+        x_codes = {}
+        x_scales = {}
+
+        def transpose_x(i):
+            words = x_rows[i].bitcast(F32)
+            xt = psum.tile([P, PASSES, 2, P], F32, tag="xt", bufs=3)
+            for g in range(PASSES):
+                for u in range(2):
+                    nc.tensor.transpose(xt[:, g, u, :], words[:, 256 * g + u : 256 * (g + 1) : 2], ident[:])
+            xg = ring.tile([P, PASSES * P * PACK], BF16, tag="xg", bufs=4, align_bytes=64)
+            nc.scalar.copy(
+                out=xg[:].bitcast(F32).rearrange("p (g r u) -> p g r u", g=PASSES, u=2),
+                in_=xt[:].rearrange("p g u r -> p g r u"),
+            )
+            x_grouped[i] = xg
+
+        def quantize_x(i):
+            xc = keep.tile([P, PASSES * P], U32, name="x_codes%d" % i, align_bytes=64)
+            xs = keep.tile([P, PASSES * P], U8, name="x_scales%d" % i, align_bytes=64)
+            nc.vector.quantize_mx(out=xc[:].bitcast(E5M2X4), scales=xs[:], in_=x_grouped[i][:])
+            x_codes[i] = xc
+            x_scales[i] = xs
+
+        w_grouped = {}
+        w_codes = {}
+        w_scales = {}
+
+        def interleave_w(c, g, src):
+            width = src.shape[2]
+            wg = ring.tile([P, width, PACK], BF16, tag="wg", bufs=3, align_bytes=64)
+            nc.vector.tensor_copy(
+                out=wg[:].rearrange("p (c i) t -> p c t i", i=4),
+                in_=src.rearrange("p t (c i) -> p c t i", i=4),
+            )
+            w_grouped[(c, g)] = wg
+
+        def quantize_w(c, g):
+            wg = w_grouped[(c, g)]
+            width = wg.shape[1]
+            wc = keep.tile([P, width], U32, name="w_codes%d_%d" % (c, g), align_bytes=64)
+            ws = keep.tile([P, width], U8, name="w_scales%d_%d" % (c, g), align_bytes=64)
+            nc.vector.quantize_mx(out=wc[:].bitcast(E4M3X4), scales=ws[:], in_=wg[:].rearrange("p w t -> p (w t)"))
+            w_codes[(c, g)] = wc
+            w_scales[(c, g)] = ws
+
+        def prepare_w(load, fillers):
+            lo, hi, g, w_raw = load
+            starts = list(range(lo, hi, CHUNK))
+            if hi - starts[-1] < CHUNK:
+                starts = starts[-1:] + starts[:-1]
+            last = None
+            for s in starts:
+                c = s // CHUNK
+                interleave_w(c, g, w_raw[:, :, s - lo : min(s + CHUNK, hi) - lo])
+                if last is not None:
+                    quantize_w(last, g)
+                last = c
+            for i in fillers:
+                quantize_x(i)
+            quantize_w(last, g)
+
+        for i in range(4):
+            transpose_x(i)
+        quantize_x(0)
+        quantize_x(1)
+        transpose_x(4)
+        transpose_x(5)
+        prepare_w(w_loaded[0], (2, 3))
+        transpose_x(6)
+        transpose_x(7)
+        prepare_w(w_loaded[1], (4, 5))
+        quantize_x(6)
+        quantize_x(7)
+        for load in w_loaded[2:]:
+            prepare_w(load, ())
+
+        def multiply(acc, i, c):
+            for g in range(PASSES):
+                cols = slice(g * P, (g + 1) * P)
+                nc.tensor.matmul_mx(
+                    out=acc,
+                    lhsT=x_codes[i][:, cols].bitcast(E5M2X4),
+                    lhsT_scale=x_scales[i][:, cols],
+                    rhs=w_codes[(c, g)][:].bitcast(E4M3X4),
+                    rhs_scale=w_scales[(c, g)][:],
+                    start=(g == 0),
+                    stop=(g == PASSES - 1),
+                )
+
+        def project(steps, first_chunk, out):
+            rows = {}
+            done = {}
+            for i, c in steps:
+                if i not in rows:
+                    row = ring.tile([P, E], F32, tag="row", bufs=12)
+                    rows[i] = row
+                    done[i] = 0
+                acc = psum.tile([P, CHUNK], F32, tag="acc", bufs=5)
+                multiply(acc[:], i, first_chunk + c)
+                nc.scalar.activation(out=rows[i][:, c * CHUNK : (c + 1) * CHUNK], in_=acc[:], func=SILU)
+                done[i] += 1
+                if done[i] == CHUNKS:
+                    nc.sync.dma_start(out=by_token(out)[:, i, :], in_=rows[i][:])
+
+        project(
+            [(i, 0) for i in range(TILES)] + [(i, c) for i in range(TILES) for c in (1, 2)],
+            0,
+            out_0,
+        )
+
+        gains = psum.tile([P, 2 * D], F32, tag="xt", bufs=3)
+        nc.tensor.matmul(gains[:], lhsT=ones[:], rhs=gain_rows[:], start=True, stop=True)
+        y = keep.tile([P, TILES, D], F32)
+        per_bank = CHUNK // D
+        for i0 in range(0, TILES, per_bank):
+            acc = psum.tile([P, per_bank, D], F32, tag="acc", bufs=5)
+            for i in range(i0, i0 + per_bank):
+                multiply(acc[:, i - i0, :], i, QK)
+            nc.scalar.activation(out=y[:, i0 : i0 + per_bank, :], in_=acc[:], func=SILU)
+
+        ahead = TILES // 2
+        project(
+            [(i, 0) for i in range(ahead)]
+            + [(i, c) for i in range(ahead) for c in (1, 2)]
+            + [(i, c) for i in range(ahead, TILES) for c in range(CHUNKS)],
+            CHUNKS,
+            out_1,
+        )
+
+        shape = [P, TILES, 2, HALF]
+        y_split = y[:].rearrange("p i (d h) -> p i h d", h=2)
+        cos_b = cos_sb[:].unsqueeze(2).broadcast_to(shape)
+        sin_b = sin_sb[:].unsqueeze(2).broadcast_to(shape)
+        scaled = []
+        for n in range(2):
+            yg = keep.tile(shape, F32, name="scaled%d" % n)
+            gain = gains[:, n * D : (n + 1) * D].rearrange("p (d h) -> p h d", h=2).unsqueeze(1).broadcast_to(shape)
+            nc.vector.tensor_tensor(out=yg[:], in0=y_split, in1=gain, op=MULT)
+            scaled.append(yg)
+        for yg, out in zip(scaled, (out_2, out_3)):
+            yc = ring.tile(shape, F32, tag="yc", bufs=1)
+            ys = ring.tile(shape, F32, tag="ys", bufs=1)
+            rot = ring.tile(shape, F32, tag="rot", bufs=2)
+            nc.vector.tensor_tensor(out=yc[:], in0=yg[:], in1=cos_b, op=MULT)
+            nc.vector.tensor_tensor(out=ys[:], in0=yg[:], in1=sin_b, op=MULT)
+            nc.vector.tensor_tensor(out=rot[:, :, 0, :], in0=yc[:, :, 0, :], in1=ys[:, :, 1, :], op=SUB)
+            nc.vector.tensor_tensor(out=rot[:, :, 1, :], in0=ys[:, :, 0, :], in1=yc[:, :, 1, :], op=ADD)
+            nc.sync.dma_start(out=by_token(out), in_=rot[:].rearrange("p i h d -> p i (h d)"))

@@ -25,8 +25,7 @@ TILES = S // P
 CHUNK = 512
 CHUNKS = E // CHUNK
 HALF = D // 2
-X_LOADS = ((0, 2), (2, 4), (4, 8))
-W_LOADS = ((0, CHUNK), (CHUNK, E), (E, 2 * E + D))
+X_HALF = TILES // 2
 QK = 2 * CHUNKS
 
 
@@ -52,20 +51,29 @@ def tile_gatedattentionunit_pa_kernel(
         nc.gpsimd.memset(gain_rows[:], 0.0)
 
         x_rows = {}
-        for lo, hi in X_LOADS:
-            x_raw = keep.tile([P, hi - lo, H], BF16, name="x_raw%d" % lo)
-            nc.sync.dma_start(out=x_raw[:], in_=by_token(hidden_states)[:, lo:hi, :])
-            for i in range(lo, hi):
-                x_rows[i] = x_raw[:, i - lo, :]
-        w_loaded = []
-        for lo, hi in W_LOADS:
-            for g in range(PASSES):
-                w_raw = keep.tile([P, PACK, hi - lo], BF16, name="w_raw%d_%d" % (lo, g))
-                nc.sync.dma_start(
-                    out=w_raw[:],
-                    in_=W_i[g * K_PASS : (g + 1) * K_PASS, lo:hi].rearrange("(p j) w -> p j w", j=PACK),
-                )
-                w_loaded.append((lo, hi, g, w_raw))
+        w_raws = {}
+
+        def load_x(lo):
+            x_raw = keep.tile([P, X_HALF, H], BF16, name="x_raw%d" % lo)
+            nc.sync.dma_start(out=x_raw[:], in_=by_token(hidden_states)[:, lo : lo + X_HALF, :])
+            for i in range(X_HALF):
+                x_rows[lo + i] = x_raw[:, i, :]
+
+        def load_w(lo, hi, g):
+            w_raw = keep.tile([P, PACK, hi - lo], BF16, name="w_raw%d_%d" % (lo, g))
+            nc.sync.dma_start(
+                out=w_raw[:],
+                in_=W_i[g * K_PASS : (g + 1) * K_PASS, lo:hi].rearrange("(p j) w -> p j w", j=PACK),
+            )
+            for s in range(lo, hi, CHUNK):
+                w_raws[(s // CHUNK, g)] = w_raw[:, :, s - lo : min(s + CHUNK, hi) - lo]
+
+        load_w(0, E, 0)
+        load_x(0)
+        load_w(0, E, 1)
+        load_x(X_HALF)
+        load_w(E, 2 * E + D, 0)
+        load_w(E, 2 * E + D, 1)
         sin_sb = keep.tile([P, TILES, HALF], BF16)
         cos_sb = keep.tile([P, TILES, HALF], BF16)
         nc.sync.dma_start(out=sin_sb[:], in_=by_token(sin))
@@ -101,10 +109,10 @@ def tile_gatedattentionunit_pa_kernel(
         w_codes = {}
         w_scales = {}
 
-        def interleave_w(c, g, src):
-            width = src.shape[2]
-            wg = ring.tile([P, width, PACK], BF16, tag="wg", bufs=3, align_bytes=64)
-            nc.vector.tensor_copy(
+        def interleave_w(c, g, copy):
+            src = w_raws[(c, g)]
+            wg = ring.tile([P, src.shape[2], PACK], BF16, tag="wg", bufs=4, align_bytes=64)
+            copy(
                 out=wg[:].rearrange("p (c i) t -> p c t i", i=4),
                 in_=src.rearrange("p t (c i) -> p c t i", i=4),
             )
@@ -119,36 +127,12 @@ def tile_gatedattentionunit_pa_kernel(
             w_codes[(c, g)] = wc
             w_scales[(c, g)] = ws
 
-        def prepare_w(load, fillers):
-            lo, hi, g, w_raw = load
-            starts = list(range(lo, hi, CHUNK))
-            if hi - starts[-1] < CHUNK:
-                starts = starts[-1:] + starts[:-1]
-            last = None
-            for s in starts:
-                c = s // CHUNK
-                interleave_w(c, g, w_raw[:, :, s - lo : min(s + CHUNK, hi) - lo])
-                if last is not None:
-                    quantize_w(last, g)
-                last = c
-            for i in fillers:
-                quantize_x(i)
-            quantize_w(last, g)
-
-        for i in range(4):
-            transpose_x(i)
-        quantize_x(0)
-        quantize_x(1)
-        transpose_x(4)
-        transpose_x(5)
-        prepare_w(w_loaded[0], (2, 3))
-        transpose_x(6)
-        transpose_x(7)
-        prepare_w(w_loaded[1], (4, 5))
-        quantize_x(6)
-        quantize_x(7)
-        for load in w_loaded[2:]:
-            prepare_w(load, ())
+        def prepare_w(units):
+            for n, unit in enumerate(units):
+                interleave_w(*unit, nc.vector.tensor_copy)
+                if n > 0:
+                    quantize_w(*units[n - 1])
+            quantize_w(*units[-1])
 
         def multiply(acc, i, c):
             for g in range(PASSES):
@@ -163,26 +147,46 @@ def tile_gatedattentionunit_pa_kernel(
                     stop=(g == PASSES - 1),
                 )
 
-        def project(steps, first_chunk, out):
-            rows = {}
-            done = {}
-            for i, c in steps:
-                if i not in rows:
-                    row = ring.tile([P, E], F32, tag="row", bufs=12)
-                    rows[i] = row
-                    done[i] = 0
-                acc = psum.tile([P, CHUNK], F32, tag="acc", bufs=5)
-                multiply(acc[:], i, first_chunk + c)
-                nc.scalar.activation(out=rows[i][:, c * CHUNK : (c + 1) * CHUNK], in_=acc[:], func=SILU)
-                done[i] += 1
-                if done[i] == CHUNKS:
-                    nc.sync.dma_start(out=by_token(out)[:, i, :], in_=rows[i][:])
+        pairs = {}
 
-        project(
-            [(i, 0) for i in range(TILES)] + [(i, c) for i in range(TILES) for c in (1, 2)],
-            0,
-            out_0,
-        )
+        def project(steps, part, out):
+            for i, c in steps:
+                if (part, i // 2) not in pairs:
+                    pair = ring.tile([P, 2, E], F32, tag="pair", bufs=6)
+                    pairs[(part, i // 2)] = pair
+                pair = pairs[(part, i // 2)]
+                acc = psum.tile([P, CHUNK], F32, tag="acc", bufs=5)
+                multiply(acc[:], i, part * CHUNKS + c)
+                nc.scalar.activation(out=pair[:, i % 2, c * CHUNK : (c + 1) * CHUNK], in_=acc[:], func=SILU)
+                if c == CHUNKS - 1:
+                    if i < 2 or i >= TILES - 2:
+                        nc.sync.dma_start(out=by_token(out)[:, i, :], in_=pair[:, i % 2, :])
+                    elif i % 2 == 1:
+                        nc.sync.dma_start(out=by_token(out)[:, i - 1 : i + 1, :], in_=pair[:])
+
+        interleave_w(0, 0, nc.vector.tensor_copy)
+        interleave_w(1, 0, nc.vector.tensor_copy)
+        interleave_w(2, 0, nc.scalar.copy)
+        for c in range(CHUNKS):
+            quantize_w(c, 0)
+        for i in range(X_HALF):
+            transpose_x(i)
+        for i in range(X_HALF - 1):
+            quantize_x(i)
+        interleave_w(0, 1, nc.vector.tensor_copy)
+        quantize_x(X_HALF - 1)
+        quantize_w(0, 1)
+        project([(i, 0) for i in range(X_HALF)], 0, out_0)
+        prepare_w([(1, 1), (2, 1)])
+        for step in range(2):
+            late = (X_HALF + 2 * step, X_HALF + 2 * step + 1)
+            for i in late:
+                transpose_x(i)
+            project([(i, c) for i in (2 * step, 2 * step + 1) for c in (1, 2)], 0, out_0)
+            for i in late:
+                quantize_x(i)
+            prepare_w([(c, step) for c in (QK, 3, 4, 5)])
+        project([(i, c) for i in range(X_HALF, TILES) for c in range(CHUNKS)], 0, out_0)
 
         gains = psum.tile([P, 2 * D], F32, tag="xt", bufs=3)
         nc.tensor.matmul(gains[:], lhsT=ones[:], rhs=gain_rows[:], start=True, stop=True)
@@ -194,15 +198,6 @@ def tile_gatedattentionunit_pa_kernel(
                 multiply(acc[:, i - i0, :], i, QK)
             nc.scalar.activation(out=y[:, i0 : i0 + per_bank, :], in_=acc[:], func=SILU)
 
-        ahead = TILES // 2
-        project(
-            [(i, 0) for i in range(ahead)]
-            + [(i, c) for i in range(ahead) for c in (1, 2)]
-            + [(i, c) for i in range(ahead, TILES) for c in range(CHUNKS)],
-            CHUNKS,
-            out_1,
-        )
-
         shape = [P, TILES, 2, HALF]
         y_split = y[:].rearrange("p i (d h) -> p i h d", h=2)
         cos_b = cos_sb[:].unsqueeze(2).broadcast_to(shape)
@@ -213,12 +208,22 @@ def tile_gatedattentionunit_pa_kernel(
             gain = gains[:, n * D : (n + 1) * D].rearrange("p (d h) -> p h d", h=2).unsqueeze(1).broadcast_to(shape)
             nc.vector.tensor_tensor(out=yg[:], in0=y_split, in1=gain, op=MULT)
             scaled.append(yg)
-        for yg, out in zip(scaled, (out_2, out_3)):
-            yc = ring.tile(shape, F32, tag="yc", bufs=1)
-            ys = ring.tile(shape, F32, tag="ys", bufs=1)
+
+        def rotate(yg, out):
+            yc = ring.tile(shape, F32, tag="wg", bufs=4, align_bytes=64)
+            ys = ring.tile(shape, F32, tag="wg", bufs=4, align_bytes=64)
             rot = ring.tile(shape, F32, tag="rot", bufs=2)
             nc.vector.tensor_tensor(out=yc[:], in0=yg[:], in1=cos_b, op=MULT)
             nc.vector.tensor_tensor(out=ys[:], in0=yg[:], in1=sin_b, op=MULT)
             nc.vector.tensor_tensor(out=rot[:, :, 0, :], in0=yc[:, :, 0, :], in1=ys[:, :, 1, :], op=SUB)
             nc.vector.tensor_tensor(out=rot[:, :, 1, :], in0=ys[:, :, 0, :], in1=yc[:, :, 1, :], op=ADD)
             nc.sync.dma_start(out=by_token(out), in_=rot[:].rearrange("p i h d -> p i (h d)"))
+
+        def v_tiles(lo, hi):
+            project([(i, c) for i in range(lo, hi) for c in range(CHUNKS)], 1, out_1)
+
+        v_tiles(0, 2)
+        rotate(scaled[0], out_2)
+        v_tiles(2, 4)
+        rotate(scaled[1], out_3)
+        v_tiles(4, TILES)

@@ -22,11 +22,17 @@ PACK = 4
 K_PASS = P * PACK
 PASSES = H // K_PASS
 TILES = S // P
+HALF_TILES = TILES // 2
 CHUNK = 512
 CHUNKS = E // CHUNK
-HALF = D // 2
-X_HALF = TILES // 2
 QK = 2 * CHUNKS
+ROT = D // 2
+
+XT_BANKS = 3
+ACC_BANKS = 5
+X_SLOTS = 4
+W_SLOTS = 4
+ROW_SLOTS = 6
 
 
 def tile_gatedattentionunit_pa_kernel(
@@ -50,14 +56,17 @@ def tile_gatedattentionunit_pa_kernel(
         gain_rows = keep.tile([P, 2 * D], BF16)
         nc.gpsimd.memset(gain_rows[:], 0.0)
 
-        x_rows = {}
-        w_raws = {}
+        warm = keep.tile([P, 1], F32)
+        nc.scalar.activation(out=warm[:], in_=ones[:, 0:1], func=SILU)
 
-        def load_x(lo):
-            x_raw = keep.tile([P, X_HALF, H], BF16, name="x_raw%d" % lo)
-            nc.sync.dma_start(out=x_raw[:], in_=by_token(hidden_states)[:, lo : lo + X_HALF, :])
-            for i in range(X_HALF):
-                x_rows[lo + i] = x_raw[:, i, :]
+        x_rows = {}
+        w_rows = {}
+
+        def load_x(first):
+            x_raw = keep.tile([P, HALF_TILES, H], BF16, name="x_raw%d" % first)
+            nc.sync.dma_start(out=x_raw[:], in_=by_token(hidden_states)[:, first : first + HALF_TILES, :])
+            for i in range(HALF_TILES):
+                x_rows[first + i] = x_raw[:, i, :]
 
         def load_w(lo, hi, g):
             w_raw = keep.tile([P, PACK, hi - lo], BF16, name="w_raw%d_%d" % (lo, g))
@@ -65,17 +74,17 @@ def tile_gatedattentionunit_pa_kernel(
                 out=w_raw[:],
                 in_=W_i[g * K_PASS : (g + 1) * K_PASS, lo:hi].rearrange("(p j) w -> p j w", j=PACK),
             )
-            for s in range(lo, hi, CHUNK):
-                w_raws[(s // CHUNK, g)] = w_raw[:, :, s - lo : min(s + CHUNK, hi) - lo]
+            for col in range(lo, hi, CHUNK):
+                w_rows[(col // CHUNK, g)] = w_raw[:, :, col - lo : min(col + CHUNK, hi) - lo]
 
-        load_w(0, E, 0)
-        load_x(0)
-        load_w(0, E, 1)
-        load_x(X_HALF)
-        load_w(E, 2 * E + D, 0)
-        load_w(E, 2 * E + D, 1)
-        sin_sb = keep.tile([P, TILES, HALF], BF16)
-        cos_sb = keep.tile([P, TILES, HALF], BF16)
+        for g in range(PASSES):
+            load_x(g * HALF_TILES)
+            load_w(0, CHUNK, g)
+        for lo, hi in ((CHUNK, E), (E, 2 * E + D)):
+            for g in range(PASSES):
+                load_w(lo, hi, g)
+        sin_sb = keep.tile([P, TILES, ROT], BF16)
+        cos_sb = keep.tile([P, TILES, ROT], BF16)
         nc.sync.dma_start(out=sin_sb[:], in_=by_token(sin))
         nc.sync.dma_start(out=cos_sb[:], in_=by_token(cos))
         nc.sync.dma_start(out=gain_rows[0:1, 0:D], in_=q_scale.rearrange("(o d) -> o d", o=1))
@@ -87,11 +96,14 @@ def tile_gatedattentionunit_pa_kernel(
 
         def transpose_x(i):
             words = x_rows[i].bitcast(F32)
-            xt = psum.tile([P, PASSES, 2, P], F32, tag="xt", bufs=3)
+            pass_words = K_PASS // 2
+            xt = psum.tile([P, PASSES, 2, P], F32, tag="xt", bufs=XT_BANKS)
             for g in range(PASSES):
                 for u in range(2):
-                    nc.tensor.transpose(xt[:, g, u, :], words[:, 256 * g + u : 256 * (g + 1) : 2], ident[:])
-            xg = ring.tile([P, PASSES * P * PACK], BF16, tag="xg", bufs=4, align_bytes=64)
+                    nc.tensor.transpose(
+                        xt[:, g, u, :], words[:, pass_words * g + u : pass_words * (g + 1) : 2], ident[:]
+                    )
+            xg = ring.tile([P, PASSES * P * PACK], BF16, tag="xg", bufs=X_SLOTS, align_bytes=64)
             nc.scalar.copy(
                 out=xg[:].bitcast(F32).rearrange("p (g r u) -> p g r u", g=PASSES, u=2),
                 in_=xt[:].rearrange("p g u r -> p g r u"),
@@ -110,11 +122,11 @@ def tile_gatedattentionunit_pa_kernel(
         w_scales = {}
 
         def interleave_w(c, g, copy):
-            src = w_raws[(c, g)]
-            wg = ring.tile([P, src.shape[2], PACK], BF16, tag="wg", bufs=4, align_bytes=64)
+            src = w_rows[(c, g)]
+            wg = ring.tile([P, src.shape[2], PACK], BF16, tag="wg", bufs=W_SLOTS, align_bytes=64)
             copy(
-                out=wg[:].rearrange("p (c i) t -> p c t i", i=4),
-                in_=src.rearrange("p t (c i) -> p c t i", i=4),
+                out=wg[:].rearrange("p (a b) t -> p a t b", b=4),
+                in_=src.rearrange("p t (a b) -> p a t b", b=4),
             )
             w_grouped[(c, g)] = wg
 
@@ -127,12 +139,39 @@ def tile_gatedattentionunit_pa_kernel(
             w_codes[(c, g)] = wc
             w_scales[(c, g)] = ws
 
-        def prepare_w(units):
-            for n, unit in enumerate(units):
-                interleave_w(*unit, nc.vector.tensor_copy)
-                if n > 0:
-                    quantize_w(*units[n - 1])
-            quantize_w(*units[-1])
+        on_vector = nc.vector.tensor_copy
+        on_scalar = nc.scalar.copy
+
+        for i in range(HALF_TILES):
+            transpose_x(i)
+        interleave_w(0, 0, on_vector)
+        quantize_x(0)
+        quantize_w(0, 0)
+        for i in range(1, HALF_TILES):
+            quantize_x(i)
+        for i in range(HALF_TILES, TILES):
+            transpose_x(i)
+        interleave_w(0, 1, on_vector)
+        quantize_x(HALF_TILES)
+        quantize_w(0, 1)
+        quantize_x(HALF_TILES + 1)
+        interleave_w(1, 0, on_vector)
+        for i in range(HALF_TILES + 2, TILES):
+            quantize_x(i)
+        interleave_w(2, 0, on_scalar)
+        quantize_w(1, 0)
+        interleave_w(1, 1, on_vector)
+        quantize_w(2, 0)
+        quantize_w(1, 1)
+        last = QK - 1
+        units = [(CHUNKS - 1, 1)]
+        units += [(c, g) for g in range(PASSES) for c in [QK] + list(range(CHUNKS, last))]
+        units += [(last, g) for g in range(PASSES)]
+        for n, unit in enumerate(units):
+            interleave_w(*unit, on_vector)
+            if n > 0:
+                quantize_w(*units[n - 1])
+        quantize_w(*units[-1])
 
         def multiply(acc, i, c):
             for g in range(PASSES):
@@ -147,83 +186,68 @@ def tile_gatedattentionunit_pa_kernel(
                     stop=(g == PASSES - 1),
                 )
 
-        pairs = {}
+        rows = {}
 
-        def project(steps, part, out):
+        def project(steps, part):
+            out = by_token((out_0, out_1)[part])
             for i, c in steps:
-                if (part, i // 2) not in pairs:
-                    pair = ring.tile([P, 2, E], F32, tag="pair", bufs=6)
-                    pairs[(part, i // 2)] = pair
-                pair = pairs[(part, i // 2)]
-                acc = psum.tile([P, CHUNK], F32, tag="acc", bufs=5)
+                if (part, i // 2) not in rows:
+                    pair = ring.tile([P, 2, E], F32, tag="pair", bufs=ROW_SLOTS)
+                    rows[(part, i // 2)] = pair
+                pair = rows[(part, i // 2)]
+                acc = psum.tile([P, CHUNK], F32, tag="acc", bufs=ACC_BANKS)
                 multiply(acc[:], i, part * CHUNKS + c)
                 nc.scalar.activation(out=pair[:, i % 2, c * CHUNK : (c + 1) * CHUNK], in_=acc[:], func=SILU)
                 if c == CHUNKS - 1:
-                    if i < 2 or i >= TILES - 2:
-                        nc.sync.dma_start(out=by_token(out)[:, i, :], in_=pair[:, i % 2, :])
+                    if part == 1 or i < 2:
+                        nc.sync.dma_start(out=out[:, i, :], in_=pair[:, i % 2, :])
                     elif i % 2 == 1:
-                        nc.sync.dma_start(out=by_token(out)[:, i - 1 : i + 1, :], in_=pair[:])
+                        nc.sync.dma_start(out=out[:, i - 1 : i + 1, :], in_=pair[:])
 
-        interleave_w(0, 0, nc.vector.tensor_copy)
-        interleave_w(1, 0, nc.vector.tensor_copy)
-        interleave_w(2, 0, nc.scalar.copy)
-        for c in range(CHUNKS):
-            quantize_w(c, 0)
-        for i in range(X_HALF):
-            transpose_x(i)
-        for i in range(X_HALF - 1):
-            quantize_x(i)
-        interleave_w(0, 1, nc.vector.tensor_copy)
-        quantize_x(X_HALF - 1)
-        quantize_w(0, 1)
-        project([(i, 0) for i in range(X_HALF)], 0, out_0)
-        prepare_w([(1, 1), (2, 1)])
-        for step in range(2):
-            late = (X_HALF + 2 * step, X_HALF + 2 * step + 1)
-            for i in late:
-                transpose_x(i)
-            project([(i, c) for i in (2 * step, 2 * step + 1) for c in (1, 2)], 0, out_0)
-            for i in late:
-                quantize_x(i)
-            prepare_w([(c, step) for c in (QK, 3, 4, 5)])
-        project([(i, c) for i in range(X_HALF, TILES) for c in range(CHUNKS)], 0, out_0)
+        def chunk_major(tiles, chunks):
+            return [(i, c) for c in chunks for i in tiles]
 
-        gains = psum.tile([P, 2 * D], F32, tag="xt", bufs=3)
+        def tile_major(tiles, chunks):
+            return [(i, c) for i in tiles for c in chunks]
+
+        project(chunk_major(range(TILES), [0]), 0)
+        project(chunk_major(range(2), range(1, CHUNKS)), 0)
+        project(tile_major(range(2, TILES), range(1, CHUNKS)), 0)
+
+        gains = psum.tile([P, 2 * D], F32, tag="xt", bufs=XT_BANKS)
         nc.tensor.matmul(gains[:], lhsT=ones[:], rhs=gain_rows[:], start=True, stop=True)
-        y = keep.tile([P, TILES, D], F32)
+        qk = keep.tile([P, TILES, D], F32)
         per_bank = CHUNK // D
-        for i0 in range(0, TILES, per_bank):
-            acc = psum.tile([P, per_bank, D], F32, tag="acc", bufs=5)
-            for i in range(i0, i0 + per_bank):
-                multiply(acc[:, i - i0, :], i, QK)
-            nc.scalar.activation(out=y[:, i0 : i0 + per_bank, :], in_=acc[:], func=SILU)
+        for first in range(0, TILES, per_bank):
+            acc = psum.tile([P, per_bank, D], F32, tag="acc", bufs=ACC_BANKS)
+            for i in range(per_bank):
+                multiply(acc[:, i, :], first + i, QK)
+            nc.scalar.activation(out=qk[:, first : first + per_bank, :], in_=acc[:], func=SILU)
 
-        shape = [P, TILES, 2, HALF]
-        y_split = y[:].rearrange("p i (d h) -> p i h d", h=2)
-        cos_b = cos_sb[:].unsqueeze(2).broadcast_to(shape)
-        sin_b = sin_sb[:].unsqueeze(2).broadcast_to(shape)
+        split = [P, TILES, 2, ROT]
+        qk_split = qk[:].rearrange("p i (d h) -> p i h d", h=2)
+        cos_b = cos_sb[:].unsqueeze(2).broadcast_to(split)
+        sin_b = sin_sb[:].unsqueeze(2).broadcast_to(split)
         scaled = []
         for n in range(2):
-            yg = keep.tile(shape, F32, name="scaled%d" % n)
-            gain = gains[:, n * D : (n + 1) * D].rearrange("p (d h) -> p h d", h=2).unsqueeze(1).broadcast_to(shape)
-            nc.vector.tensor_tensor(out=yg[:], in0=y_split, in1=gain, op=MULT)
-            scaled.append(yg)
+            y = keep.tile(split, F32, name="scaled%d" % n)
+            gain = gains[:, n * D : (n + 1) * D].rearrange("p (d h) -> p h d", h=2).unsqueeze(1).broadcast_to(split)
+            nc.vector.tensor_tensor(out=y[:], in0=qk_split, in1=gain, op=MULT)
+            scaled.append(y)
 
-        def rotate(yg, out):
-            yc = ring.tile(shape, F32, tag="wg", bufs=4, align_bytes=64)
-            ys = ring.tile(shape, F32, tag="wg", bufs=4, align_bytes=64)
-            rot = ring.tile(shape, F32, tag="rot", bufs=2)
-            nc.vector.tensor_tensor(out=yc[:], in0=yg[:], in1=cos_b, op=MULT)
-            nc.vector.tensor_tensor(out=ys[:], in0=yg[:], in1=sin_b, op=MULT)
-            nc.vector.tensor_tensor(out=rot[:, :, 0, :], in0=yc[:, :, 0, :], in1=ys[:, :, 1, :], op=SUB)
-            nc.vector.tensor_tensor(out=rot[:, :, 1, :], in0=ys[:, :, 0, :], in1=yc[:, :, 1, :], op=ADD)
+        def rotate(y, out):
+            y_cos = ring.tile(split, F32, tag="wg", bufs=W_SLOTS, align_bytes=64)
+            y_sin = ring.tile(split, F32, tag="wg", bufs=W_SLOTS, align_bytes=64)
+            rot = ring.tile(split, F32, tag="rot", bufs=2)
+            nc.vector.tensor_tensor(out=y_cos[:], in0=y[:], in1=cos_b, op=MULT)
+            nc.vector.tensor_tensor(out=y_sin[:], in0=y[:], in1=sin_b, op=MULT)
+            nc.vector.tensor_tensor(out=rot[:, :, 0, :], in0=y_cos[:, :, 0, :], in1=y_sin[:, :, 1, :], op=SUB)
+            nc.vector.tensor_tensor(out=rot[:, :, 1, :], in0=y_sin[:, :, 0, :], in1=y_cos[:, :, 1, :], op=ADD)
             nc.sync.dma_start(out=by_token(out), in_=rot[:].rearrange("p i h d -> p i (h d)"))
 
-        def v_tiles(lo, hi):
-            project([(i, c) for i in range(lo, hi) for c in range(CHUNKS)], 1, out_1)
-
-        v_tiles(0, 2)
+        project(chunk_major(range(2), range(CHUNKS)), 1)
+        project(tile_major(range(2, 4), range(CHUNKS)), 1)
         rotate(scaled[0], out_2)
-        v_tiles(2, 4)
+        project(tile_major(range(4, 6), range(CHUNKS)), 1)
         rotate(scaled[1], out_3)
-        v_tiles(4, TILES)
+        project(tile_major(range(6, TILES), range(CHUNKS)), 1)

@@ -32,6 +32,7 @@ XT_BANKS = 3
 ACC_BANKS = 5
 X_SLOTS = 4
 W_SLOTS = 4
+ALIGN = 256
 ROW_SLOTS = 6
 
 
@@ -56,20 +57,17 @@ def tile_gatedattentionunit_pa_kernel(
         gain_rows = keep.tile([P, 2 * D], BF16)
         nc.gpsimd.memset(gain_rows[:], 0.0)
 
-        warm = keep.tile([P, 1], F32)
-        nc.scalar.activation(out=warm[:], in_=ones[:, 0:1], func=SILU)
-
         x_rows = {}
         w_rows = {}
 
         def load_x(first):
-            x_raw = keep.tile([P, HALF_TILES, H], BF16, name="x_raw%d" % first)
+            x_raw = keep.tile([P, HALF_TILES, H], BF16, name="x_raw%d" % first, align_bytes=ALIGN)
             nc.sync.dma_start(out=x_raw[:], in_=by_token(hidden_states)[:, first : first + HALF_TILES, :])
             for i in range(HALF_TILES):
                 x_rows[first + i] = x_raw[:, i, :]
 
         def load_w(lo, hi, g):
-            w_raw = keep.tile([P, PACK, hi - lo], BF16, name="w_raw%d_%d" % (lo, g))
+            w_raw = keep.tile([P, PACK, hi - lo], BF16, name="w_raw%d_%d" % (lo, g), align_bytes=ALIGN)
             nc.sync.dma_start(
                 out=w_raw[:],
                 in_=W_i[g * K_PASS : (g + 1) * K_PASS, lo:hi].rearrange("(p j) w -> p j w", j=PACK),
@@ -83,8 +81,8 @@ def tile_gatedattentionunit_pa_kernel(
         for lo, hi in ((CHUNK, E), (E, 2 * E + D)):
             for g in range(PASSES):
                 load_w(lo, hi, g)
-        sin_sb = keep.tile([P, TILES, ROT], BF16)
-        cos_sb = keep.tile([P, TILES, ROT], BF16)
+        sin_sb = keep.tile([P, TILES, ROT], BF16, align_bytes=ALIGN)
+        cos_sb = keep.tile([P, TILES, ROT], BF16, align_bytes=ALIGN)
         nc.sync.dma_start(out=sin_sb[:], in_=by_token(sin))
         nc.sync.dma_start(out=cos_sb[:], in_=by_token(cos))
         nc.sync.dma_start(out=gain_rows[0:1, 0:D], in_=q_scale.rearrange("(o d) -> o d", o=1))
@@ -103,7 +101,7 @@ def tile_gatedattentionunit_pa_kernel(
                     nc.tensor.transpose(
                         xt[:, g, u, :], words[:, pass_words * g + u : pass_words * (g + 1) : 2], ident[:]
                     )
-            xg = ring.tile([P, PASSES * P * PACK], BF16, tag="xg", bufs=X_SLOTS, align_bytes=64)
+            xg = ring.tile([P, PASSES * P * PACK], BF16, tag="xg", bufs=X_SLOTS, align_bytes=ALIGN)
             nc.scalar.copy(
                 out=xg[:].bitcast(F32).rearrange("p (g r u) -> p g r u", g=PASSES, u=2),
                 in_=xt[:].rearrange("p g u r -> p g r u"),
@@ -111,8 +109,8 @@ def tile_gatedattentionunit_pa_kernel(
             x_grouped[i] = xg
 
         def quantize_x(i):
-            xc = keep.tile([P, PASSES * P], U32, name="x_codes%d" % i, align_bytes=64)
-            xs = keep.tile([P, PASSES * P], U8, name="x_scales%d" % i, align_bytes=64)
+            xc = keep.tile([P, PASSES * P], U32, name="x_codes%d" % i, align_bytes=ALIGN)
+            xs = keep.tile([P, PASSES * P], U8, name="x_scales%d" % i, align_bytes=ALIGN)
             nc.vector.quantize_mx(out=xc[:].bitcast(E5M2X4), scales=xs[:], in_=x_grouped[i][:])
             x_codes[i] = xc
             x_scales[i] = xs
@@ -123,7 +121,7 @@ def tile_gatedattentionunit_pa_kernel(
 
         def interleave_w(c, g, copy):
             src = w_rows[(c, g)]
-            wg = ring.tile([P, src.shape[2], PACK], BF16, tag="wg", bufs=W_SLOTS, align_bytes=64)
+            wg = ring.tile([P, src.shape[2], PACK], BF16, tag="wg", bufs=W_SLOTS, align_bytes=ALIGN)
             copy(
                 out=wg[:].rearrange("p (a b) t -> p a t b", b=4),
                 in_=src.rearrange("p t (a b) -> p a t b", b=4),
@@ -133,8 +131,8 @@ def tile_gatedattentionunit_pa_kernel(
         def quantize_w(c, g):
             wg = w_grouped[(c, g)]
             width = wg.shape[1]
-            wc = keep.tile([P, width], U32, name="w_codes%d_%d" % (c, g), align_bytes=64)
-            ws = keep.tile([P, width], U8, name="w_scales%d_%d" % (c, g), align_bytes=64)
+            wc = keep.tile([P, width], U32, name="w_codes%d_%d" % (c, g), align_bytes=ALIGN)
+            ws = keep.tile([P, width], U8, name="w_scales%d_%d" % (c, g), align_bytes=ALIGN)
             nc.vector.quantize_mx(out=wc[:].bitcast(E4M3X4), scales=ws[:], in_=wg[:].rearrange("p w t -> p (w t)"))
             w_codes[(c, g)] = wc
             w_scales[(c, g)] = ws
@@ -192,7 +190,7 @@ def tile_gatedattentionunit_pa_kernel(
             out = by_token((out_0, out_1)[part])
             for i, c in steps:
                 if (part, i // 2) not in rows:
-                    pair = ring.tile([P, 2, E], F32, tag="pair", bufs=ROW_SLOTS)
+                    pair = ring.tile([P, 2, E], F32, tag="pair", bufs=ROW_SLOTS, align_bytes=ALIGN)
                     rows[(part, i // 2)] = pair
                 pair = rows[(part, i // 2)]
                 acc = psum.tile([P, CHUNK], F32, tag="acc", bufs=ACC_BANKS)
@@ -236,9 +234,9 @@ def tile_gatedattentionunit_pa_kernel(
             scaled.append(y)
 
         def rotate(y, out):
-            y_cos = ring.tile(split, F32, tag="wg", bufs=W_SLOTS, align_bytes=64)
-            y_sin = ring.tile(split, F32, tag="wg", bufs=W_SLOTS, align_bytes=64)
-            rot = ring.tile(split, F32, tag="rot", bufs=2)
+            y_cos = ring.tile(split, F32, tag="wg", bufs=W_SLOTS, align_bytes=ALIGN)
+            y_sin = ring.tile(split, F32, tag="wg", bufs=W_SLOTS, align_bytes=ALIGN)
+            rot = ring.tile(split, F32, tag="rot", bufs=2, align_bytes=ALIGN)
             nc.vector.tensor_tensor(out=y_cos[:], in0=y[:], in1=cos_b, op=MULT)
             nc.vector.tensor_tensor(out=y_sin[:], in0=y[:], in1=sin_b, op=MULT)
             nc.vector.tensor_tensor(out=rot[:, :, 0, :], in0=y_cos[:, :, 0, :], in1=y_sin[:, :, 1, :], op=SUB)

from contextlib import ExitStack

import concourse.mybir as mybir
from concourse.masks import make_identity

S, H, E, D = 1024, 1024, 1536, 128
FLOPS = 2 * S * H * (2 * E + D)

F32 = mybir.dt.float32
BF16 = mybir.dt.bfloat16
U32 = mybir.dt.uint32
U8 = mybir.dt.uint8
E4M3X4 = mybir.dt.float8_e4m3fn_x4
E5M2X4 = mybir.dt.float8_e5m2_x4
SILU = mybir.ActivationFunctionType.Silu
MULT = mybir.AluOpType.mult
ADD = mybir.AluOpType.add
SUB = mybir.AluOpType.subtract

P = 128
PACK = 4
K_PASS = P * PACK
PASSES = H // K_PASS
TILES = S // P
HALF_TILES = TILES // 2
CHUNK = 512
CHUNKS = E // CHUNK
QK = 2 * CHUNKS
ROT = D // 2

XT_BANKS = 3
ACC_BANKS = 5
X_SLOTS = 4
W_SLOTS = 4
ALIGN = 256
ROW_SLOTS = 6


def tile_gatedattentionunit_pa_kernel(
    tc, hidden_states, sin, cos, W_i, q_scale, k_scale, out_0, out_1, out_2, out_3
):
    nc = tc.nc

    def by_token(ap):
        return ap.flatten_outer_dims().rearrange("(p i) c -> p i c", i=TILES)

    with ExitStack() as ctx:
        keep = ctx.enter_context(tc.tile_pool(name="keep", bufs=1))
        ring = ctx.enter_context(tc.tile_pool(name="ring", bufs=1))
        psum = ctx.enter_context(tc.psum_pool(name="psum", bufs=1))
        ctx.enter_context(tc.manual_schedule())

        ident = keep.tile([P, P], F32)
        make_identity(nc, ident[:])
        ones = keep.tile([P, P], BF16)
        nc.gpsimd.memset(ones[:], 1.0)
        gain_rows = keep.tile([P, 2 * D], BF16)
        nc.gpsimd.memset(gain_rows[:], 0.0)

        x_rows = {}
        w_rows = {}

        def load_x(first):
            x_raw = keep.tile([P, HALF_TILES, H], BF16, name="x_raw%d" % first, align_bytes=ALIGN)
            nc.sync.dma_start(out=x_raw[:], in_=by_token(hidden_states)[:, first : first + HALF_TILES, :])
            for i in range(HALF_TILES):
                x_rows[first + i] = x_raw[:, i, :]

        def load_w(lo, hi, g):
            w_raw = keep.tile([P, PACK, hi - lo], BF16, name="w_raw%d_%d" % (lo, g), align_bytes=ALIGN)
            nc.sync.dma_start(
                out=w_raw[:],
                in_=W_i[g * K_PASS : (g + 1) * K_PASS, lo:hi].rearrange("(p j) w -> p j w", j=PACK),
            )
            for col in range(lo, hi, CHUNK):
                w_rows[(col // CHUNK, g)] = w_raw[:, :, col - lo : min(col + CHUNK, hi) - lo]

        for g in range(PASSES):
            load_x(g * HALF_TILES)
            load_w(0, CHUNK, g)
        for lo, hi in ((CHUNK, E), (E, 2 * E + D)):
            for g in range(PASSES):
                load_w(lo, hi, g)
        sin_sb = keep.tile([P, TILES, ROT], BF16, align_bytes=ALIGN)
        cos_sb = keep.tile([P, TILES, ROT], BF16, align_bytes=ALIGN)
        nc.sync.dma_start(out=sin_sb[:], in_=by_token(sin))
        nc.sync.dma_start(out=cos_sb[:], in_=by_token(cos))
        nc.sync.dma_start(out=gain_rows[0:1, 0:D], in_=q_scale.rearrange("(o d) -> o d", o=1))
        nc.sync.dma_start(out=gain_rows[0:1, D : 2 * D], in_=k_scale.rearrange("(o d) -> o d", o=1))

        x_grouped = {}
        x_codes = {}
        x_scales = {}

        def transpose_x(i):
            words = x_rows[i].bitcast(F32)
            pass_words = K_PASS // 2
            xt = psum.tile([P, PASSES, 2, P], F32, tag="xt", bufs=XT_BANKS)
            for g in range(PASSES):
                for u in range(2):
                    nc.tensor.transpose(
                        xt[:, g, u, :], words[:, pass_words * g + u : pass_words * (g + 1) : 2], ident[:]
                    )
            xg = ring.tile([P, PASSES * P * PACK], BF16, tag="xg", bufs=X_SLOTS, align_bytes=ALIGN)
            nc.scalar.copy(
                out=xg[:].bitcast(F32).rearrange("p (g r u) -> p g r u", g=PASSES, u=2),
                in_=xt[:].rearrange("p g u r -> p g r u"),
            )
            x_grouped[i] = xg

        def quantize_x(i):
            xc = keep.tile([P, PASSES * P], U32, name="x_codes%d" % i, align_bytes=ALIGN)
            xs = keep.tile([P, PASSES * P], U8, name="x_scales%d" % i, align_bytes=ALIGN)
            nc.vector.quantize_mx(out=xc[:].bitcast(E5M2X4), scales=xs[:], in_=x_grouped[i][:])
            x_codes[i] = xc
            x_scales[i] = xs

        w_grouped = {}
        w_codes = {}
        w_scales = {}

        def interleave_w(c, g, copy):
            src = w_rows[(c, g)]
            wg = ring.tile([P, src.shape[2], PACK], BF16, tag="wg", bufs=W_SLOTS, align_bytes=ALIGN)
            copy(
                out=wg[:].rearrange("p (a b) t -> p a t b", b=4),
                in_=src.rearrange("p t (a b) -> p a t b", b=4),
            )
            w_grouped[(c, g)] = wg

        def quantize_w(c, g):
            wg = w_grouped[(c, g)]
            width = wg.shape[1]
            wc = keep.tile([P, width], U32, name="w_codes%d_%d" % (c, g), align_bytes=ALIGN)
            ws = keep.tile([P, width], U8, name="w_scales%d_%d" % (c, g), align_bytes=ALIGN)
            nc.vector.quantize_mx(out=wc[:].bitcast(E4M3X4), scales=ws[:], in_=wg[:].rearrange("p w t -> p (w t)"))
            w_codes[(c, g)] = wc
            w_scales[(c, g)] = ws

        on_vector = nc.vector.tensor_copy
        on_scalar = nc.scalar.copy

        for i in range(HALF_TILES):
            transpose_x(i)
        interleave_w(0, 0, on_vector)
        quantize_x(0)
        quantize_w(0, 0)
        for i in range(1, HALF_TILES):
            quantize_x(i)
        for i in range(HALF_TILES, TILES):
            transpose_x(i)
        interleave_w(0, 1, on_vector)
        quantize_x(HALF_TILES)
        quantize_w(0, 1)
        quantize_x(HALF_TILES + 1)
        interleave_w(1, 0, on_vector)
        for i in range(HALF_TILES + 2, TILES):
            quantize_x(i)
        interleave_w(2, 0, on_scalar)
        quantize_w(1, 0)
        interleave_w(1, 1, on_vector)
        quantize_w(2, 0)
        quantize_w(1, 1)
        last = QK - 1
        units = [(CHUNKS - 1, 1)]
        units += [(c, g) for g in range(PASSES) for c in [QK] + list(range(CHUNKS, last))]
        units += [(last, g) for g in range(PASSES)]
        for n, unit in enumerate(units):
            interleave_w(*unit, on_vector)
            if n > 0:
                quantize_w(*units[n - 1])
        quantize_w(*units[-1])

        def multiply(acc, i, c):
            for g in range(PASSES):
                cols = slice(g * P, (g + 1) * P)
                nc.tensor.matmul_mx(
                    out=acc,
                    lhsT=x_codes[i][:, cols].bitcast(E5M2X4),
                    lhsT_scale=x_scales[i][:, cols],
                    rhs=w_codes[(c, g)][:].bitcast(E4M3X4),
                    rhs_scale=w_scales[(c, g)][:],
                    start=(g == 0),
                    stop=(g == PASSES - 1),
                )

        rows = {}

        def project(steps, part):
            out = by_token((out_0, out_1)[part])
            for i, c in steps:
                if (part, i // 2) not in rows:
                    pair = ring.tile([P, 2, E], F32, tag="pair", bufs=ROW_SLOTS, align_bytes=ALIGN)
                    rows[(part, i // 2)] = pair
                pair = rows[(part, i // 2)]
                acc = psum.tile([P, CHUNK], F32, tag="acc", bufs=ACC_BANKS)
                multiply(acc[:], i, part * CHUNKS + c)
                nc.scalar.activation(out=pair[:, i % 2, c * CHUNK : (c + 1) * CHUNK], in_=acc[:], func=SILU)
                if c == CHUNKS - 1:
                    if part == 1 or i < 2:
                        nc.sync.dma_start(out=out[:, i, :], in_=pair[:, i % 2, :])
                    elif i % 2 == 1:
                        nc.sync.dma_start(out=out[:, i - 1 : i + 1, :], in_=pair[:])

        def chunk_major(tiles, chunks):
            return [(i, c) for c in chunks for i in tiles]

        def tile_major(tiles, chunks):
            return [(i, c) for i in tiles for c in chunks]

        project(chunk_major(range(TILES), [0]), 0)
        project(chunk_major(range(2), range(1, CHUNKS)), 0)
        project(tile_major(range(2, TILES), range(1, CHUNKS)), 0)

        gains = psum.tile([P, 2 * D], F32, tag="xt", bufs=XT_BANKS)
        nc.tensor.matmul(gains[:], lhsT=ones[:], rhs=gain_rows[:], start=True, stop=True)
        qk = keep.tile([P, TILES, D], F32)
        per_bank = CHUNK // D
        for first in range(0, TILES, per_bank):
            acc = psum.tile([P, per_bank, D], F32, tag="acc", bufs=ACC_BANKS)
            for i in range(per_bank):
                multiply(acc[:, i, :], first + i, QK)
            nc.scalar.activation(out=qk[:, first : first + per_bank, :], in_=acc[:], func=SILU)

        split = [P, TILES, 2, ROT]
        qk_split = qk[:].rearrange("p i (d h) -> p i h d", h=2)
        cos_b = cos_sb[:].unsqueeze(2).broadcast_to(split)
        sin_b = sin_sb[:].unsqueeze(2).broadcast_to(split)
        scaled = []
        for n in range(2):
            y = keep.tile(split, F32, name="scaled%d" % n)
            gain = gains[:, n * D : (n + 1) * D].rearrange("p (d h) -> p h d", h=2).unsqueeze(1).broadcast_to(split)
            nc.vector.tensor_tensor(out=y[:], in0=qk_split, in1=gain, op=MULT)
            scaled.append(y)

        def rotate(y, out):
            y_cos = ring.tile(split, F32, tag="wg", bufs=W_SLOTS, align_bytes=ALIGN)
            y_sin = ring.tile(split, F32, tag="wg", bufs=W_SLOTS, align_bytes=ALIGN)
            rot = ring.tile(split, F32, tag="rot", bufs=2, align_bytes=ALIGN)
            nc.vector.tensor_tensor(out=y_cos[:], in0=y[:], in1=cos_b, op=MULT)
            nc.vector.tensor_tensor(out=y_sin[:], in0=y[:], in1=sin_b, op=MULT)
            nc.vector.tensor_tensor(out=rot[:, :, 0, :], in0=y_cos[:, :, 0, :], in1=y_sin[:, :, 1, :], op=SUB)
            nc.vector.tensor_tensor(out=rot[:, :, 1, :], in0=y_sin[:, :, 0, :], in1=y_cos[:, :, 1, :], op=ADD)
            nc.sync.dma_start(out=by_token(out), in_=rot[:].rearrange("p i h d -> p i (h d)"))

        project(chunk_major(range(2), range(CHUNKS)), 1)
        project(tile_major(range(2, 4), range(CHUNKS)), 1)
        rotate(scaled[0], out_2)
        project(tile_major(range(4, 6), range(CHUNKS)), 1)
        rotate(scaled[1], out_3)
        project(tile_major(range(6, TILES), range(CHUNKS)), 1)
